import numpy as np
import ml_dtypes


def mxq(x, axis, fmt="e4m3"):
    dtype, down = {"e4m3": (ml_dtypes.float8_e4m3fn, 7), "e5m2": (ml_dtypes.float8_e5m2, 14)}[fmt]
    v = np.moveaxis(np.asarray(x, np.float32).astype(ml_dtypes.bfloat16).astype(np.float64), axis, -1)
    blocks = v.reshape(v.shape[:-1] + (-1, 32))
    amax = np.abs(blocks).max(-1, keepdims=True)
    byte = np.maximum(np.where(amax > 0, np.frexp(amax)[1] - 1 + 127, 0) - down, 1)
    scale = np.exp2(byte - 127.0)
    codes = (blocks / scale).astype(np.float32).astype(dtype).astype(np.float64)
    return np.moveaxis((codes * scale).reshape(v.shape), -1, axis)


WIDE = False


def mx_kscale(k):
    if not WIDE:
        return np.ones(k)
    levels = np.array([10, -10, 5, -5, 0])
    if k % 512:
        return np.exp2(np.random.permutation(np.resize(levels, k // 32))).repeat(32)
    a = np.empty((k // 512, 16))
    for p in range(k // 512):
        a[p, :8] = np.random.permutation(np.resize(levels, 8))
        for g in range(8):
            far = levels[np.abs(levels - a[p, g]) >= 10]
            a[p, g + 8] = far[np.random.randint(len(far))]
    return np.exp2(a.ravel()).repeat(32)


BF16 = ml_dtypes.bfloat16


def bf(x):
    return np.asarray(x, np.float32).astype(BF16)


def f64(x):
    return np.asarray(x).astype(np.float64)


B, H0, C0, C1, C2, NA, NO = 6, 32, 512, 512, 1024, 4, 128
H1, H2 = H0 // 2, H0 // 4
O = NA * NO
P0 = H0 * H0
T = B * P0
R0 = NA * P0
R = NA * (H0 * H0 + H1 * H1 + H2 * H2)


def sigmoid(v):
    return 1.0 / (1.0 + np.exp(-v))


def _draw_level(c, h):
    f = bf(np.random.standard_normal((B, c, h, h)))
    w = bf(np.random.standard_normal((O, c)) / np.sqrt(c))
    b = bf(np.random.standard_normal(O) * 0.5)
    return f, w, b


def setup_inputs():
    s = mx_kscale(T).reshape(B, P0)
    u = mx_kscale(O)
    f00, w00, b0 = _draw_level(C0, H0)
    f1, w1, b1 = _draw_level(C1, H1)
    f2, w2, b2 = _draw_level(C2, H2)
    anchors = bf(1.0 + 4.0 * np.random.random((3, NA, 2)))
    fac = np.ones((B, R, NO))
    fac[:, :R0] = (u.reshape(1, NA, 1, NO) / s.reshape(B, 1, P0, 1)).reshape(B, R0, NO)
    g = bf(np.random.standard_normal((B, R, NO)) * np.exp2(np.random.randint(-6, 1, (B, R, 1))) * fac)
    wb = f64(w00).reshape(NA, NO, C0)[:, :4, :].reshape(NA * 4, C0)
    bb = f64(b0).reshape(NA, NO)[:, :4].reshape(NA * 4)
    z = wb @ f64(f00).reshape(B, C0, P0) + bb[None, :, None]
    z0 = z.reshape(B, NA, 4, P0).transpose(0, 1, 3, 2).reshape(B, R0, 4)
    f0 = bf(f64(f00) * s.reshape(B, 1, H0, H0))
    w0 = bf(f64(w00) / u[:, None])
    return {"f0": f0, "f1": f1, "f2": f2, "w0": w0, "b0": b0, "w1": w1, "b1": b1, "w2": w2, "b2": b2,
            "anchors": anchors, "z0": np.asarray(z0, np.float32), "grad_out": g}


def reference(f0, f1, f2, w0, b0, w1, b1, w2, b2, anchors, z0, grad_out):
    g = f64(grad_out)[:, :R0, :]
    sg = sigmoid(f64(z0))
    a0 = np.repeat(f64(anchors)[0], P0, axis=0)
    dxy = g[..., 0:2] * (2.0 * sg[..., 0:2] * (1.0 - sg[..., 0:2]))
    dwh = g[..., 2:4] * (8.0 * np.square(sg[..., 2:4]) * (1.0 - sg[..., 2:4])) * a0[None]
    dy = np.concatenate([dxy, dwh, g[..., 4:]], axis=-1)
    dy = dy.reshape(B, NA, P0, NO).transpose(0, 1, 3, 2).reshape(B, O, P0)
    dy = dy
    df = mxq(f64(w0), 0, "e4m3").T @ mxq(dy, 1, "e5m2")
    dyt = dy.transpose(1, 0, 2).reshape(O, T)
    ft = f64(f0).reshape(B, C0, P0).transpose(1, 0, 2).reshape(C0, T)
    dw = mxq(dyt, 1, "e5m2") @ mxq(ft, 1, "e4m3").T
    return df.reshape(B, C0, H0, H0), dw

@@ -1,0 +1,273 @@
+from contextlib import ExitStack
+
+import concourse.mybir as mybir
+from concourse.masks import make_identity
+
+B, C0, O, P0 = 6, 512, 512, 1024
+T = B * P0
+FLOPS = 2 * (2 * T * O * C0)
+BYTES = 2 * (B * C0 * P0) + 2 * (O * C0) + 16 + 4 * (B * 4096 * 4) + 2 * (B * 4096 * 128) + 4 * (B * C0 * P0) + 4 * (O * C0)
+
+F32 = mybir.dt.float32
+BF16 = mybir.dt.bfloat16
+U32 = mybir.dt.uint32
+U8 = mybir.dt.uint8
+E4 = mybir.dt.float8_e4m3fn_x4
+E5 = mybir.dt.float8_e5m2_x4
+ALU = mybir.AluOpType
+ACT = mybir.ActivationFunctionType
+
+P = 128
+PASSES = T // 512
+G_BUFS = 8
+F_BUFS = 4
+
+
+def tile_head_t_v_kernel(tc, f0, f1, f2, w0, b0, w1, b1, w2, b2, anchors, z0, grad_out, out_0, out_1):
+    nc = tc.nc
+    with ExitStack() as ctx:
+        const = ctx.enter_context(tc.tile_pool(name="const", bufs=1))
+        gpool = ctx.enter_context(tc.tile_pool(name="gpool", bufs=G_BUFS))
+        fpool = ctx.enter_context(tc.tile_pool(name="fpool", bufs=F_BUFS))
+        spool = ctx.enter_context(tc.tile_pool(name="spool", bufs=2))
+        grp = ctx.enter_context(tc.tile_pool(name="grp", bufs=2))
+        cpool = ctx.enter_context(tc.tile_pool(name="cpool", bufs=3))
+        opool = ctx.enter_context(tc.tile_pool(name="opool", bufs=3))
+        accp = ctx.enter_context(tc.psum_pool(name="accp", bufs=1))
+        rot = ctx.enter_context(tc.psum_pool(name="rot", bufs=4))
+
+        g_view = grad_out[:, 0:4096, :].rearrange("n (a g p jj) j -> n g p a (jj j)", a=4, g=2, p=P, jj=4)
+        z_view = z0.rearrange("n (a g p jj) f -> p (n a g) (jj f)", a=4, g=2, p=P, jj=4)
+        f_view = f0.rearrange("n (m cc) u v -> n m (cc u v)", cc=4)
+        o0_view = out_0.rearrange("n (m ct) u v -> n m ct (u v)", ct=4)
+
+        graw = {}
+        fraw = {}
+        gsort = {}
+        grp_a = {}
+        grp_b = {}
+        grp_f = {}
+        q_a = {}
+        q_b = {}
+        q_f = {}
+        stage = {}
+
+        zt = const.tile([P, 768], F32, name="zt")
+        sg = const.tile([P, 768], F32, name="sg")
+        om = const.tile([P, 768], F32, name="om")
+        fac = const.tile([P, 768], F32, name="fac")
+        cst = const.tile([P, 128], F32, name="cst")
+        ancb = const.tile([P, 8], BF16, name="ancb")
+        warm = const.tile([P, 8], F32, name="warm")
+        warm2 = const.tile([P, 8], F32, name="warm2")
+        ident = const.tile([P, P], F32, name="ident")
+        w_raw = const.tile([P, 4, 512], BF16, name="w_raw")
+        w_grp = const.tile([P, 2048], BF16, name="w_grp", align_bytes=64)
+        w_codes = const.tile([P, 512], U32, name="w_codes", align_bytes=64)
+        w_scales = const.tile([P, 512], U8, name="w_scales", align_bytes=64)
+        o1 = const.tile([P, 4, 512], F32, name="o1")
+
+        def load_z(c_lo, c_hi):
+            nc.sync.dma_start(
+                out=zt[:].rearrange("p (c x) -> p c x", x=16)[:, c_lo:c_hi, :], in_=z_view[:, c_lo:c_hi, :]
+            )
+
+        def load_g(i):
+            n, g = divmod(i, 2)
+            graw[i] = gpool.tile([P, 4, 4, 128], BF16, name="graw")
+            nc.sync.dma_start(out=graw[i][:].rearrange("p a jj j -> p a (jj j)"), in_=g_view[n, g])
+
+        def load_f(n):
+            fraw[n] = fpool.tile([P, 4096], BF16, name="fraw")
+            nc.sync.dma_start(out=fraw[n][:], in_=f_view[n])
+
+        def factors(n_lo, n_hi):
+            lo, hi, nn = 128 * n_lo, 128 * n_hi, n_hi - n_lo
+            nc.scalar.activation(out=sg[:, lo:hi], in_=zt[:, lo:hi], func=ACT.Sigmoid)
+            nc.scalar.activation(out=om[:, lo:hi], in_=zt[:, lo:hi], func=ACT.Sigmoid, scale=-1.0)
+            nc.vector.tensor_tensor(out=om[:, lo:hi], in0=om[:, lo:hi], in1=sg[:, lo:hi], op=ALU.mult)
+            nc.vector.tensor_tensor(
+                out=fac[:, lo:hi].rearrange("p (n x) -> p n x", x=128),
+                in0=om[:, lo:hi].rearrange("p (n x) -> p n x", x=128),
+                in1=cst[:].unsqueeze(1).to_broadcast([P, nn, 128]),
+                op=ALU.mult,
+            )
+            nc.vector.tensor_tensor(
+                out=fac[:, lo:hi].rearrange("p (r f) -> p r f", f=4)[:, :, 2:4],
+                in0=fac[:, lo:hi].rearrange("p (r f) -> p r f", f=4)[:, :, 2:4],
+                in1=sg[:, lo:hi].rearrange("p (r f) -> p r f", f=4)[:, :, 2:4],
+                op=ALU.mult,
+            )
+
+        def fix(i):
+            n, g = divmod(i, 2)
+            fac6 = fac[:].rearrange("p (n a g jj f) -> p n a g jj f", n=B, a=4, g=2, jj=4, f=4)
+            nc.vector.tensor_tensor(
+                out=graw[i][:, :, :, 0:4], in0=graw[i][:, :, :, 0:4], in1=fac6[:, n, :, g, :, :], op=ALU.mult
+            )
+
+        def sort(i):
+            gsort[i] = spool.tile([P, 2048], BF16, name="gsort")
+            nc.vector.tensor_copy(
+                out=gsort[i][:].bitcast(F32).rearrange("p (jj u a jq) -> p jj u a jq", jj=4, u=2, a=4, jq=32),
+                in_=graw[i][:]
+                .rearrange("p a jj j -> p (a jj j)")
+                .bitcast(F32)
+                .rearrange("p (a jj jq u) -> p jj u a jq", a=4, jj=4, jq=32, u=2),
+            )
+
+        def weave(i):
+            grp_a[i] = grp.tile([P, 2048], BF16, name="grp_a", align_bytes=64)
+            nc.vector.tensor_copy(
+                out=grp_a[i][:].rearrange("p (a j jj) -> p a j jj", a=4, j=128, jj=4),
+                in_=graw[i][:].rearrange("p a jj j -> p a j jj"),
+            )
+
+        def quantize(src, fmt, label):
+            codes = cpool.tile([P, 512], U32, name="codes_%s" % label, align_bytes=64)
+            scales = cpool.tile([P, 512], U8, name="scales_%s" % label, align_bytes=64)
+            nc.vector.quantize_mx(out=codes[:].bitcast(fmt), scales=scales[:], in_=src[:])
+            return codes, scales
+
+        def transpose_d(i):
+            grp_b[i] = grp.tile([P, 2048], BF16, name="grp_b", align_bytes=64)
+            words = gsort[i][:].bitcast(F32)
+            dst = grp_b[i][:].bitcast(F32).rearrange("q (p h x) -> q h p x", p=P, h=2, x=4)
+            for h in range(2):
+                bank = rot.tile([P, 512], F32, name="bank")
+                for x in range(4):
+                    k = 4 * h + x
+                    nc.tensor.transpose(bank[:, 128 * x : 128 * (x + 1)], words[:, 128 * k : 128 * (k + 1)], ident[:])
+                nc.scalar.copy(out=dst[:, h], in_=bank[:].rearrange("q (x p) -> q p x", x=4))
+
+        def transpose_f(i):
+            n, g = divmod(i, 2)
+            grp_f[i] = grp.tile([P, 2048], BF16, name="grp_f", align_bytes=64)
+            words = fraw[n][:].bitcast(F32)
+            dst = grp_f[i][:].bitcast(F32)
+            for h in range(2):
+                bank = rot.tile([P, 512], F32, name="bank")
+                for x in range(4):
+                    cc, u = 2 * h + x // 2, x % 2
+                    lo = 512 * cc + 256 * g
+                    nc.tensor.transpose(bank[:, 128 * x : 128 * (x + 1)], words[:, lo + u : lo + 256 : 2], ident[:])
+                nc.scalar.copy(
+                    out=dst[:, 512 * h : 512 * (h + 1)].rearrange("p (cl m u) -> p cl m u", cl=2, m=P, u=2),
+                    in_=bank[:].rearrange("p (cl u m) -> p cl m u", cl=2, u=2, m=P),
+                )
+
+        def mm1(i):
+            for a in range(4):
+                cols = slice(128 * a, 128 * (a + 1))
+                nc.tensor.matmul_mx(
+                    out=acc[a][:],
+                    lhsT=q_a[i][0][:, cols].bitcast(E5),
+                    lhsT_scale=q_a[i][1][:, cols],
+                    rhs=q_f[i][0][:].bitcast(E4),
+                    rhs_scale=q_f[i][1][:],
+                    start=(i == 0),
+                    stop=(i == PASSES - 1),
+                )
+
+        def mm0(i):
+            n, g = divmod(i, 2)
+            if g == 0:
+                stage[n] = opool.tile([P, 4, 1024], F32, name="stage")
+            for ct in range(4):
+                cols = slice(128 * ct, 128 * (ct + 1))
+                bank = rot.tile([P, 512], F32, name="bank")
+                nc.tensor.matmul_mx(
+                    out=bank[:],
+                    lhsT=w_codes[:, cols].bitcast(E4),
+                    lhsT_scale=w_scales[:, cols],
+                    rhs=q_b[i][0][:].bitcast(E5),
+                    rhs_scale=q_b[i][1][:],
+                    start=True,
+                    stop=True,
+                )
+                nc.scalar.copy(out=stage[n][:, ct, 512 * g : 512 * (g + 1)], in_=bank[:])
+                if n == B - 1 and ct % 2 == 1:
+                    nc.sync.dma_start(
+                        out=o0_view[n, :, ct - 1 : ct + 1, 512 * g : 512 * (g + 1)],
+                        in_=stage[n][:, ct - 1 : ct + 1, 512 * g : 512 * (g + 1)],
+                    )
+            if n < B - 1 and g == 1:
+                nc.sync.dma_start(out=o0_view[n], in_=stage[n][:])
+
+        nc.scalar.dma_start(out=ancb[:], in_=anchors[0].rearrange("a w -> (a w)").partition_broadcast(P))
+        load_z(0, 8)
+        load_g(0)
+        nc.sync.dma_start(out=w_raw[:], in_=w0.rearrange("(p j) c -> p j c", j=4))
+        load_f(0)
+        load_g(1)
+        load_z(8, 16)
+        load_g(2)
+        load_g(3)
+        load_f(1)
+        load_z(16, 48)
+        load_g(4)
+        load_g(5)
+        load_f(2)
+        load_g(6)
+        load_g(7)
+        load_f(3)
+
+        nc.vector.memset(warm[:], 0.0)
+        nc.scalar.activation(out=warm2[:], in_=warm[:], func=ACT.Sigmoid)
+        make_identity(nc, ident[:])
+        nc.vector.memset(cst[:], 2.0)
+        nc.vector.tensor_scalar(
+            out=cst[:].rearrange("p (a x f) -> p a x f", a=4, x=8, f=4)[:, :, :, 2:4],
+            in0=ancb[:].rearrange("p (a w) -> p a w", w=2).unsqueeze(2).to_broadcast([P, 4, 8, 2]),
+            scalar1=8.0,
+            scalar2=None,
+            op0=ALU.mult,
+        )
+        acc = {}
+        for a in range(4):
+            acc[a] = accp.tile([P, 512], F32, name="acc%d" % a)
+
+        factors(0, 1)
+        fix(0)
+        sort(0)
+        nc.vector.tensor_copy(
+            out=w_grp[:].rearrange("p (ct m j) -> p ct m j", ct=4, m=P, j=4),
+            in_=w_raw[:].rearrange("p j (m ct) -> p ct m j", ct=4),
+        )
+        weave(0)
+        nc.vector.quantize_mx(out=w_codes[:].bitcast(E4), scales=w_scales[:], in_=w_grp[:])
+
+        for i in range(PASSES + 1):
+            if i < PASSES:
+                transpose_d(i)
+                transpose_f(i)
+            if i == 0:
+                factors(1, 2)
+            if i == 2:
+                factors(2, B)
+            if i + 1 < PASSES:
+                fix(i + 1)
+            if i < PASSES:
+                q_a[i] = quantize(grp_a[i], E5, "a")
+            if i + 1 < PASSES:
+                sort(i + 1)
+            if i < PASSES:
+                q_b[i] = quantize(grp_b[i], E5, "b")
+            if i + 1 < PASSES:
+                weave(i + 1)
+            if i < PASSES:
+                q_f[i] = quantize(grp_f[i], E4, "f")
+            if i >= 1:
+                mm1(i - 1)
+                if i == PASSES:
+                    for a in range(4):
+                        nc.vector.tensor_copy(
+                            out=o1[:, a, :].rearrange("j (m cc) -> j m cc", cc=4),
+                            in_=acc[a][:].rearrange("j (cc m) -> j m cc", cc=4),
+                        )
+                        nc.sync.dma_start(out=out_1[128 * a : 128 * (a + 1), :], in_=o1[:, a, :])
+                mm0(i - 1)
+            if i + G_BUFS < PASSES:
+                load_g(i + G_BUFS)
+            if i % 2 == 1 and i // 2 + F_BUFS < B:
+                load_f(i // 2 + F_BUFS)

@@ -19,8 +19,10 @@ ACT = mybir.ActivationFunctionType
 
 P = 128
 PASSES = T // 512
-G_BUFS = 8
+G_BUFS = 9
 F_BUFS = 4
+VSHARE = 2
+WHOLE_IMAGES = 5
 
 
 def tile_head_t_v_kernel(tc, f0, f1, f2, w0, b0, w1, b1, w2, b2, anchors, z0, grad_out, out_0, out_1):
@@ -33,6 +35,7 @@ def tile_head_t_v_kernel(tc, f0, f1, f2, w0, b0, w1, b1, w2, b2, anchors, z0, gr
         grp = ctx.enter_context(tc.tile_pool(name="grp", bufs=2))
         cpool = ctx.enter_context(tc.tile_pool(name="cpool", bufs=3))
         opool = ctx.enter_context(tc.tile_pool(name="opool", bufs=3))
+        tailp = ctx.enter_context(tc.tile_pool(name="tailp", bufs=4))
         accp = ctx.enter_context(tc.psum_pool(name="accp", bufs=1))
         rot = ctx.enter_context(tc.psum_pool(name="rot", bufs=4))
 
@@ -81,23 +84,24 @@ def tile_head_t_v_kernel(tc, f0, f1, f2, w0, b0, w1, b1, w2, b2, anchors, z0, gr
             fraw[n] = fpool.tile([P, 4096], BF16, name="fraw")
             nc.sync.dma_start(out=fraw[n][:], in_=f_view[n])
 
-        def factors(n_lo, n_hi):
-            lo, hi, nn = 128 * n_lo, 128 * n_hi, n_hi - n_lo
+        def factors_scalar(n_lo, n_hi):
+            lo, hi = 128 * n_lo, 128 * n_hi
             nc.scalar.activation(out=sg[:, lo:hi], in_=zt[:, lo:hi], func=ACT.Sigmoid)
             nc.scalar.activation(out=om[:, lo:hi], in_=zt[:, lo:hi], func=ACT.Sigmoid, scale=-1.0)
-            nc.vector.tensor_tensor(out=om[:, lo:hi], in0=om[:, lo:hi], in1=sg[:, lo:hi], op=ALU.mult)
-            nc.vector.tensor_tensor(
-                out=fac[:, lo:hi].rearrange("p (n x) -> p n x", x=128),
-                in0=om[:, lo:hi].rearrange("p (n x) -> p n x", x=128),
-                in1=cst[:].unsqueeze(1).to_broadcast([P, nn, 128]),
-                op=ALU.mult,
-            )
-            nc.vector.tensor_tensor(
-                out=fac[:, lo:hi].rearrange("p (r f) -> p r f", f=4)[:, :, 2:4],
-                in0=fac[:, lo:hi].rearrange("p (r f) -> p r f", f=4)[:, :, 2:4],
-                in1=sg[:, lo:hi].rearrange("p (r f) -> p r f", f=4)[:, :, 2:4],
-                op=ALU.mult,
-            )
+
+        def factors_vector(n, part):
+            lo, hi = 128 * n, 128 * (n + 1)
+            if part == 0:
+                nc.vector.tensor_tensor(out=om[:, lo:hi], in0=om[:, lo:hi], in1=sg[:, lo:hi], op=ALU.mult)
+            if part == 1:
+                nc.vector.tensor_tensor(out=fac[:, lo:hi], in0=om[:, lo:hi], in1=cst[:], op=ALU.mult)
+            if part == 2:
+                nc.vector.tensor_tensor(
+                    out=fac[:, lo:hi].rearrange("p (r f) -> p r f", f=4)[:, :, 2:4],
+                    in0=fac[:, lo:hi].rearrange("p (r f) -> p r f", f=4)[:, :, 2:4],
+                    in1=sg[:, lo:hi].rearrange("p (r f) -> p r f", f=4)[:, :, 2:4],
+                    op=ALU.mult,
+                )
 
         def fix(i):
             n, g = divmod(i, 2)
@@ -116,9 +120,9 @@ def tile_head_t_v_kernel(tc, f0, f1, f2, w0, b0, w1, b1, w2, b2, anchors, z0, gr
                 .rearrange("p (a jj jq u) -> p jj u a jq", a=4, jj=4, jq=32, u=2),
             )
 
-        def weave(i):
+        def weave(i, copy):
             grp_a[i] = grp.tile([P, 2048], BF16, name="grp_a", align_bytes=64)
-            nc.vector.tensor_copy(
+            copy(
                 out=grp_a[i][:].rearrange("p (a j jj) -> p a j jj", a=4, j=128, jj=4),
                 in_=graw[i][:].rearrange("p a jj j -> p a j jj"),
             )
@@ -171,7 +175,8 @@ def tile_head_t_v_kernel(tc, f0, f1, f2, w0, b0, w1, b1, w2, b2, anchors, z0, gr
 
         def mm0(i):
             n, g = divmod(i, 2)
-            if g == 0:
+            whole = n < WHOLE_IMAGES
+            if whole and g == 0:
                 stage[n] = opool.tile([P, 4, 1024], F32, name="stage")
             for ct in range(4):
                 cols = slice(128 * ct, 128 * (ct + 1))
@@ -185,32 +190,62 @@ def tile_head_t_v_kernel(tc, f0, f1, f2, w0, b0, w1, b1, w2, b2, anchors, z0, gr
                     start=True,
                     stop=True,
                 )
-                nc.scalar.copy(out=stage[n][:, ct, 512 * g : 512 * (g + 1)], in_=bank[:])
-                if n == B - 1 and ct % 2 == 1:
-                    nc.sync.dma_start(
-                        out=o0_view[n, :, ct - 1 : ct + 1, 512 * g : 512 * (g + 1)],
-                        in_=stage[n][:, ct - 1 : ct + 1, 512 * g : 512 * (g + 1)],
-                    )
-            if n < B - 1 and g == 1:
+                copy = nc.vector.tensor_copy if vector_empties(i, ct) else nc.scalar.copy
+                if whole:
+                    copy(out=stage[n][:, ct, 512 * g : 512 * (g + 1)], in_=bank[:])
+                else:
+                    if ct % 2 == 0:
+                        piece = tailp.tile([P, 2, 512], F32, name="piece")
+                    copy(out=piece[:, ct % 2, :], in_=bank[:])
+                    if ct % 2 == 1:
+                        nc.sync.dma_start(out=o0_view[n, :, ct - 1 : ct + 1, 512 * g : 512 * (g + 1)], in_=piece[:])
+            if whole and g == 1:
                 nc.sync.dma_start(out=o0_view[n], in_=stage[n][:])
 
+        def evacuate_out1(a, engine_copy):
+            engine_copy(
+                out=o1[:, a, :].rearrange("j (m cc) -> j m cc", cc=4),
+                in_=acc[a][:].rearrange("j (cc m) -> j m cc", cc=4),
+            )
+            nc.sync.dma_start(out=out_1[128 * a : 128 * (a + 1), :], in_=o1[:, a, :])
+
+        def prepare_w_weave():
+            nc.vector.tensor_copy(
+                out=w_grp[:].rearrange("p (ct m j) -> p ct m j", ct=4, m=P, j=4),
+                in_=w_raw[:].rearrange("p j (m ct) -> p ct m j", ct=4),
+            )
+
+        def prepare_w_quant():
+            nc.vector.quantize_mx(out=w_codes[:].bitcast(E4), scales=w_scales[:], in_=w_grp[:])
+
+        acc = {}
+        for a in range(4):
+            acc[a] = accp.tile([P, 512], F32, name="acc%d" % a)
+
+        def vector_empties(i, ct):
+            return ct == 3 and (i % VSHARE == 0 or i >= PASSES - 2)
+
+        ctx.enter_context(tc.manual_schedule())
         nc.scalar.dma_start(out=ancb[:], in_=anchors[0].rearrange("a w -> (a w)").partition_broadcast(P))
         load_z(0, 8)
         load_g(0)
         nc.sync.dma_start(out=w_raw[:], in_=w0.rearrange("(p j) c -> p j c", j=4))
-        load_f(0)
         load_g(1)
+        load_f(0)
         load_z(8, 16)
         load_g(2)
         load_g(3)
+        load_z(16, 24)
         load_f(1)
-        load_z(16, 48)
         load_g(4)
         load_g(5)
+        load_z(24, 32)
         load_f(2)
         load_g(6)
         load_g(7)
+        load_z(32, 48)
         load_f(3)
+        load_g(8)
 
         nc.vector.memset(warm[:], 0.0)
         nc.scalar.activation(out=warm2[:], in_=warm[:], func=ACT.Sigmoid)
@@ -223,51 +258,61 @@ def tile_head_t_v_kernel(tc, f0, f1, f2, w0, b0, w1, b1, w2, b2, anchors, z0, gr
             scalar2=None,
             op0=ALU.mult,
         )
-        acc = {}
-        for a in range(4):
-            acc[a] = accp.tile([P, 512], F32, name="acc%d" % a)
-
-        factors(0, 1)
+        factors_scalar(0, 1)
+        for part in range(3):
+            factors_vector(0, part)
         fix(0)
         sort(0)
-        nc.vector.tensor_copy(
-            out=w_grp[:].rearrange("p (ct m j) -> p ct m j", ct=4, m=P, j=4),
-            in_=w_raw[:].rearrange("p j (m ct) -> p ct m j", ct=4),
-        )
-        weave(0)
-        nc.vector.quantize_mx(out=w_codes[:].bitcast(E4), scales=w_scales[:], in_=w_grp[:])
+        weave(0, nc.scalar.copy)
+        prepare_w_weave()
+        fix(1)
+        sort(1)
+        prepare_w_quant()
 
-        for i in range(PASSES + 1):
-            if i < PASSES:
-                transpose_d(i)
+        def live(k):
+            return 0 <= k < PASSES
+
+        for i in range(-1, PASSES):
+            n_next = (i + 3) // 2
+            new_image = i % 2 == 1 and n_next < B
+            if live(i + 1):
+                transpose_d(i + 1)
+            if i == 0:
+                factors_scalar(1, 2)
+            if new_image:
+                factors_scalar(n_next, n_next + 1)
+            if live(i):
                 transpose_f(i)
             if i == 0:
-                factors(1, 2)
-            if i == 2:
-                factors(2, B)
-            if i + 1 < PASSES:
-                fix(i + 1)
-            if i < PASSES:
-                q_a[i] = quantize(grp_a[i], E5, "a")
-            if i + 1 < PASSES:
-                sort(i + 1)
-            if i < PASSES:
-                q_b[i] = quantize(grp_b[i], E5, "b")
-            if i + 1 < PASSES:
-                weave(i + 1)
-            if i < PASSES:
+                for part in range(3):
+                    factors_vector(1, part)
+                fix(2)
+            if live(i + 1):
+                q_b[i + 1] = quantize(grp_b[i + 1], E5, "b")
+            if new_image:
+                factors_vector(n_next, 0)
+            if live(i + 2) and i >= 0:
+                sort(i + 2)
+            if new_image:
+                factors_vector(n_next, 1)
+            if live(i):
                 q_f[i] = quantize(grp_f[i], E4, "f")
-            if i >= 1:
+            if new_image:
+                factors_vector(n_next, 2)
+            if live(i):
+                q_a[i] = quantize(grp_a[i], E5, "a")
+            if live(i - 1):
                 mm1(i - 1)
-                if i == PASSES:
-                    for a in range(4):
-                        nc.vector.tensor_copy(
-                            out=o1[:, a, :].rearrange("j (m cc) -> j m cc", cc=4),
-                            in_=acc[a][:].rearrange("j (cc m) -> j m cc", cc=4),
-                        )
-                        nc.sync.dma_start(out=out_1[128 * a : 128 * (a + 1), :], in_=o1[:, a, :])
-                mm0(i - 1)
-            if i + G_BUFS < PASSES:
-                load_g(i + G_BUFS)
-            if i % 2 == 1 and i // 2 + F_BUFS < B:
+            if live(i):
+                mm0(i)
+            if live(i + 3) and i >= 0:
+                fix(i + 3)
+            if live(i + 1) and i >= 0:
+                weave(i + 1, nc.vector.tensor_copy)
+            if i + 1 + G_BUFS < PASSES:
+                load_g(i + 1 + G_BUFS)
+            if i % 2 == 1 and live(i) and i // 2 + F_BUFS < B:
                 load_f(i // 2 + F_BUFS)
+        mm1(PASSES - 1)
+        for a in range(4):
+            evacuate_out1(a, nc.vector.tensor_copy if a % 2 == 0 else nc.scalar.copy)

@@ -160,18 +160,20 @@ def tile_head_t_v_kernel(tc, f0, f1, f2, w0, b0, w1, b1, w2, b2, anchors, z0, gr
                     in_=bank[:].rearrange("p (cl u m) -> p cl m u", cl=2, u=2, m=P),
                 )
 
-        def mm1(i):
-            for a in range(4):
-                cols = slice(128 * a, 128 * (a + 1))
-                nc.tensor.matmul_mx(
-                    out=acc[a][:],
-                    lhsT=q_a[i][0][:, cols].bitcast(E5),
-                    lhsT_scale=q_a[i][1][:, cols],
-                    rhs=q_f[i][0][:].bitcast(E4),
-                    rhs_scale=q_f[i][1][:],
-                    start=(i == 0),
-                    stop=(i == PASSES - 1),
-                )
+        def mm1(i, a):
+            cols = slice(128 * a, 128 * (a + 1))
+            nc.tensor.matmul_mx(
+                out=acc[a][:],
+                lhsT=q_a[i][0][:, cols].bitcast(E5),
+                lhsT_scale=q_a[i][1][:, cols],
+                rhs=q_f[i][0][:].bitcast(E4),
+                rhs_scale=q_f[i][1][:],
+                start=(i == 0),
+                stop=(i == PASSES - 1),
+            )
+
+        def live(k):
+            return 0 <= k < PASSES
 
         def mm0(i):
             n, g = divmod(i, 2)
@@ -190,6 +192,8 @@ def tile_head_t_v_kernel(tc, f0, f1, f2, w0, b0, w1, b1, w2, b2, anchors, z0, gr
                     start=True,
                     stop=True,
                 )
+                if live(i - 1):
+                    mm1(i - 1, ct)
                 copy = nc.vector.tensor_copy if vector_empties(i, ct) else nc.scalar.copy
                 if whole:
                     copy(out=stage[n][:, ct, 512 * g : 512 * (g + 1)], in_=bank[:])
@@ -269,9 +273,6 @@ def tile_head_t_v_kernel(tc, f0, f1, f2, w0, b0, w1, b1, w2, b2, anchors, z0, gr
         sort(1)
         prepare_w_quant()
 
-        def live(k):
-            return 0 <= k < PASSES
-
         for i in range(-1, PASSES):
             n_next = (i + 3) // 2
             new_image = i % 2 == 1 and n_next < B
@@ -301,8 +302,6 @@ def tile_head_t_v_kernel(tc, f0, f1, f2, w0, b0, w1, b1, w2, b2, anchors, z0, gr
                 factors_vector(n_next, 2)
             if live(i):
                 q_a[i] = quantize(grp_a[i], E5, "a")
-            if live(i - 1):
-                mm1(i - 1)
             if live(i):
                 mm0(i)
             if live(i + 3) and i >= 0:
@@ -313,6 +312,7 @@ def tile_head_t_v_kernel(tc, f0, f1, f2, w0, b0, w1, b1, w2, b2, anchors, z0, gr
                 load_g(i + 1 + G_BUFS)
             if i % 2 == 1 and live(i) and i // 2 + F_BUFS < B:
                 load_f(i // 2 + F_BUFS)
-        mm1(PASSES - 1)
+        for a in range(4):
+            mm1(PASSES - 1, a)
         for a in range(4):
             evacuate_out1(a, nc.vector.tensor_copy if a % 2 == 0 else nc.scalar.copy)

@@ -275,11 +275,11 @@ def tile_head_t_v_kernel(tc, f0, f1, f2, w0, b0, w1, b1, w2, b2, anchors, z0, gr
 
         for i in range(-1, PASSES):
             n_next = (i + 3) // 2
-            new_image = i % 2 == 1 and n_next < B
-            if live(i + 1):
-                transpose_d(i + 1)
+            new_image = i >= 1 and i % 2 == 1 and n_next < B
             if i == 0:
                 factors_scalar(1, 2)
+            if live(i + 1):
+                transpose_d(i + 1)
             if new_image:
                 factors_scalar(n_next, n_next + 1)
             if live(i):

@@ -122,10 +122,16 @@ def tile_head_t_v_kernel(tc, f0, f1, f2, w0, b0, w1, b1, w2, b2, anchors, z0, gr
 
         def weave(i, copy):
             grp_a[i] = grp.tile([P, 2048], BF16, name="grp_a", align_bytes=64)
-            copy(
-                out=grp_a[i][:].rearrange("p (a j jj) -> p a j jj", a=4, j=128, jj=4),
-                in_=graw[i][:].rearrange("p a jj j -> p a j jj"),
-            )
+            if i == 0:
+                copy(
+                    out=grp_a[i][:].rearrange("p (a j jj) -> p a j jj", a=4, j=128, jj=4),
+                    in_=graw[i][:].rearrange("p a jj j -> p a j jj"),
+                )
+            else:
+                copy(
+                    out=grp_a[i][:].rearrange("p (a c r jj) -> p a c jj r", a=4, c=32, r=4, jj=4),
+                    in_=graw[i][:].rearrange("p a jj (c r) -> p a c jj r", r=4),
+                )
 
         def quantize(src, fmt, label):
             codes = cpool.tile([P, 512], U32, name="codes_%s" % label, align_bytes=64)

from contextlib import ExitStack

import concourse.mybir as mybir
from concourse.masks import make_identity

B, C0, O, P0 = 6, 512, 512, 1024
T = B * P0
FLOPS = 2 * (2 * T * O * C0)
BYTES = 2 * (B * C0 * P0) + 2 * (O * C0) + 16 + 4 * (B * 4096 * 4) + 2 * (B * 4096 * 128) + 4 * (B * C0 * P0) + 4 * (O * C0)

F32 = mybir.dt.float32
BF16 = mybir.dt.bfloat16
U32 = mybir.dt.uint32
U8 = mybir.dt.uint8
E4 = mybir.dt.float8_e4m3fn_x4
E5 = mybir.dt.float8_e5m2_x4
ALU = mybir.AluOpType
ACT = mybir.ActivationFunctionType

P = 128
PASSES = T // 512
G_BUFS = 9
F_BUFS = 4
VSHARE = 2
WHOLE_IMAGES = 5


def tile_head_t_v_kernel(tc, f0, f1, f2, w0, b0, w1, b1, w2, b2, anchors, z0, grad_out, out_0, out_1):
    nc = tc.nc
    with ExitStack() as ctx:
        const = ctx.enter_context(tc.tile_pool(name="const", bufs=1))
        gpool = ctx.enter_context(tc.tile_pool(name="gpool", bufs=G_BUFS))
        fpool = ctx.enter_context(tc.tile_pool(name="fpool", bufs=F_BUFS))
        spool = ctx.enter_context(tc.tile_pool(name="spool", bufs=2))
        grp = ctx.enter_context(tc.tile_pool(name="grp", bufs=2))
        cpool = ctx.enter_context(tc.tile_pool(name="cpool", bufs=3))
        opool = ctx.enter_context(tc.tile_pool(name="opool", bufs=3))
        tailp = ctx.enter_context(tc.tile_pool(name="tailp", bufs=4))
        accp = ctx.enter_context(tc.psum_pool(name="accp", bufs=1))
        rot = ctx.enter_context(tc.psum_pool(name="rot", bufs=4))

        g_view = grad_out[:, 0:4096, :].rearrange("n (a g p jj) j -> n g p a (jj j)", a=4, g=2, p=P, jj=4)
        z_view = z0.rearrange("n (a g p jj) f -> p (n a g) (jj f)", a=4, g=2, p=P, jj=4)
        f_view = f0.rearrange("n (m cc) u v -> n m (cc u v)", cc=4)
        o0_view = out_0.rearrange("n (m ct) u v -> n m ct (u v)", ct=4)

        graw = {}
        fraw = {}
        gsort = {}
        grp_a = {}
        grp_b = {}
        grp_f = {}
        q_a = {}
        q_b = {}
        q_f = {}
        stage = {}

        zt = const.tile([P, 768], F32, name="zt")
        sg = const.tile([P, 768], F32, name="sg")
        om = const.tile([P, 768], F32, name="om")
        fac = const.tile([P, 768], F32, name="fac")
        cst = const.tile([P, 128], F32, name="cst")
        ancb = const.tile([P, 8], BF16, name="ancb")
        warm = const.tile([P, 8], F32, name="warm")
        warm2 = const.tile([P, 8], F32, name="warm2")
        ident = const.tile([P, P], F32, name="ident")
        w_raw = const.tile([P, 4, 512], BF16, name="w_raw")
        w_grp = const.tile([P, 2048], BF16, name="w_grp", align_bytes=64)
        w_codes = const.tile([P, 512], U32, name="w_codes", align_bytes=64)
        w_scales = const.tile([P, 512], U8, name="w_scales", align_bytes=64)
        o1 = const.tile([P, 4, 512], F32, name="o1")

        def load_z(c_lo, c_hi):
            nc.sync.dma_start(
                out=zt[:].rearrange("p (c x) -> p c x", x=16)[:, c_lo:c_hi, :], in_=z_view[:, c_lo:c_hi, :]
            )

        def load_g(i):
            n, g = divmod(i, 2)
            graw[i] = gpool.tile([P, 4, 4, 128], BF16, name="graw")
            nc.sync.dma_start(out=graw[i][:].rearrange("p a jj j -> p a (jj j)"), in_=g_view[n, g])

        def load_f(n):
            fraw[n] = fpool.tile([P, 4096], BF16, name="fraw")
            nc.sync.dma_start(out=fraw[n][:], in_=f_view[n])

        def factors_scalar(n_lo, n_hi):
            lo, hi = 128 * n_lo, 128 * n_hi
            nc.scalar.activation(out=sg[:, lo:hi], in_=zt[:, lo:hi], func=ACT.Sigmoid)
            nc.scalar.activation(out=om[:, lo:hi], in_=zt[:, lo:hi], func=ACT.Sigmoid, scale=-1.0)

        def factors_vector(n, part):
            lo, hi = 128 * n, 128 * (n + 1)
            if part == 0:
                nc.vector.tensor_tensor(out=om[:, lo:hi], in0=om[:, lo:hi], in1=sg[:, lo:hi], op=ALU.mult)
            if part == 1:
                nc.vector.tensor_tensor(out=fac[:, lo:hi], in0=om[:, lo:hi], in1=cst[:], op=ALU.mult)
            if part == 2:
                nc.vector.tensor_tensor(
                    out=fac[:, lo:hi].rearrange("p (r f) -> p r f", f=4)[:, :, 2:4],
                    in0=fac[:, lo:hi].rearrange("p (r f) -> p r f", f=4)[:, :, 2:4],
                    in1=sg[:, lo:hi].rearrange("p (r f) -> p r f", f=4)[:, :, 2:4],
                    op=ALU.mult,
                )

        def fix(i):
            n, g = divmod(i, 2)
            fac6 = fac[:].rearrange("p (n a g jj f) -> p n a g jj f", n=B, a=4, g=2, jj=4, f=4)
            nc.vector.tensor_tensor(
                out=graw[i][:, :, :, 0:4], in0=graw[i][:, :, :, 0:4], in1=fac6[:, n, :, g, :, :], op=ALU.mult
            )

        def sort(i):
            gsort[i] = spool.tile([P, 2048], BF16, name="gsort")
            nc.vector.tensor_copy(
                out=gsort[i][:].bitcast(F32).rearrange("p (jj u a jq) -> p jj u a jq", jj=4, u=2, a=4, jq=32),
                in_=graw[i][:]
                .rearrange("p a jj j -> p (a jj j)")
                .bitcast(F32)
                .rearrange("p (a jj jq u) -> p jj u a jq", a=4, jj=4, jq=32, u=2),
            )

        def weave(i, copy):
            grp_a[i] = grp.tile([P, 2048], BF16, name="grp_a", align_bytes=64)
            if i == 0:
                copy(
                    out=grp_a[i][:].rearrange("p (a j jj) -> p a j jj", a=4, j=128, jj=4),
                    in_=graw[i][:].rearrange("p a jj j -> p a j jj"),
                )
            else:
                copy(
                    out=grp_a[i][:].rearrange("p (a c r jj) -> p a c jj r", a=4, c=32, r=4, jj=4),
                    in_=graw[i][:].rearrange("p a jj (c r) -> p a c jj r", r=4),
                )

        def quantize(src, fmt, label):
            codes = cpool.tile([P, 512], U32, name="codes_%s" % label, align_bytes=64)
            scales = cpool.tile([P, 512], U8, name="scales_%s" % label, align_bytes=64)
            nc.vector.quantize_mx(out=codes[:].bitcast(fmt), scales=scales[:], in_=src[:])
            return codes, scales

        def transpose_d(i):
            grp_b[i] = grp.tile([P, 2048], BF16, name="grp_b", align_bytes=64)
            words = gsort[i][:].bitcast(F32)
            dst = grp_b[i][:].bitcast(F32).rearrange("q (p h x) -> q h p x", p=P, h=2, x=4)
            for h in range(2):
                bank = rot.tile([P, 512], F32, name="bank")
                for x in range(4):
                    k = 4 * h + x
                    nc.tensor.transpose(bank[:, 128 * x : 128 * (x + 1)], words[:, 128 * k : 128 * (k + 1)], ident[:])
                nc.scalar.copy(out=dst[:, h], in_=bank[:].rearrange("q (x p) -> q p x", x=4))

        def transpose_f(i):
            n, g = divmod(i, 2)
            grp_f[i] = grp.tile([P, 2048], BF16, name="grp_f", align_bytes=64)
            words = fraw[n][:].bitcast(F32)
            dst = grp_f[i][:].bitcast(F32)
            for h in range(2):
                bank = rot.tile([P, 512], F32, name="bank")
                for x in range(4):
                    cc, u = 2 * h + x // 2, x % 2
                    lo = 512 * cc + 256 * g
                    nc.tensor.transpose(bank[:, 128 * x : 128 * (x + 1)], words[:, lo + u : lo + 256 : 2], ident[:])
                nc.scalar.copy(
                    out=dst[:, 512 * h : 512 * (h + 1)].rearrange("p (cl m u) -> p cl m u", cl=2, m=P, u=2),
                    in_=bank[:].rearrange("p (cl u m) -> p cl m u", cl=2, u=2, m=P),
                )

        def mm1(i, a):
            cols = slice(128 * a, 128 * (a + 1))
            nc.tensor.matmul_mx(
                out=acc[a][:],
                lhsT=q_a[i][0][:, cols].bitcast(E5),
                lhsT_scale=q_a[i][1][:, cols],
                rhs=q_f[i][0][:].bitcast(E4),
                rhs_scale=q_f[i][1][:],
                start=(i == 0),
                stop=(i == PASSES - 1),
            )

        def live(k):
            return 0 <= k < PASSES

        def mm0(i):
            n, g = divmod(i, 2)
            whole = n < WHOLE_IMAGES
            if whole and g == 0:
                stage[n] = opool.tile([P, 4, 1024], F32, name="stage")
            for ct in range(4):
                cols = slice(128 * ct, 128 * (ct + 1))
                bank = rot.tile([P, 512], F32, name="bank")
                nc.tensor.matmul_mx(
                    out=bank[:],
                    lhsT=w_codes[:, cols].bitcast(E4),
                    lhsT_scale=w_scales[:, cols],
                    rhs=q_b[i][0][:].bitcast(E5),
                    rhs_scale=q_b[i][1][:],
                    start=True,
                    stop=True,
                )
                if live(i - 1):
                    mm1(i - 1, ct)
                copy = nc.vector.tensor_copy if vector_empties(i, ct) else nc.scalar.copy
                if whole:
                    copy(out=stage[n][:, ct, 512 * g : 512 * (g + 1)], in_=bank[:])
                else:
                    if ct % 2 == 0:
                        piece = tailp.tile([P, 2, 512], F32, name="piece")
                    copy(out=piece[:, ct % 2, :], in_=bank[:])
                    if ct % 2 == 1:
                        nc.sync.dma_start(out=o0_view[n, :, ct - 1 : ct + 1, 512 * g : 512 * (g + 1)], in_=piece[:])
            if whole and g == 1:
                nc.sync.dma_start(out=o0_view[n], in_=stage[n][:])

        def evacuate_out1(a, engine_copy):
            engine_copy(
                out=o1[:, a, :].rearrange("j (m cc) -> j m cc", cc=4),
                in_=acc[a][:].rearrange("j (cc m) -> j m cc", cc=4),
            )
            nc.sync.dma_start(out=out_1[128 * a : 128 * (a + 1), :], in_=o1[:, a, :])

        def prepare_w_weave():
            nc.vector.tensor_copy(
                out=w_grp[:].rearrange("p (ct m j) -> p ct m j", ct=4, m=P, j=4),
                in_=w_raw[:].rearrange("p j (m ct) -> p ct m j", ct=4),
            )

        def prepare_w_quant():
            nc.vector.quantize_mx(out=w_codes[:].bitcast(E4), scales=w_scales[:], in_=w_grp[:])

        acc = {}
        for a in range(4):
            acc[a] = accp.tile([P, 512], F32, name="acc%d" % a)

        def vector_empties(i, ct):
            return ct == 3 and (i % VSHARE == 0 or i >= PASSES - 2)

        ctx.enter_context(tc.manual_schedule())
        nc.scalar.dma_start(out=ancb[:], in_=anchors[0].rearrange("a w -> (a w)").partition_broadcast(P))
        load_z(0, 8)
        load_g(0)
        nc.sync.dma_start(out=w_raw[:], in_=w0.rearrange("(p j) c -> p j c", j=4))
        load_g(1)
        load_f(0)
        load_z(8, 16)
        load_g(2)
        load_g(3)
        load_z(16, 24)
        load_f(1)
        load_g(4)
        load_g(5)
        load_z(24, 32)
        load_f(2)
        load_g(6)
        load_g(7)
        load_z(32, 48)
        load_f(3)
        load_g(8)

        nc.vector.memset(warm[:], 0.0)
        nc.scalar.activation(out=warm2[:], in_=warm[:], func=ACT.Sigmoid)
        make_identity(nc, ident[:])
        nc.vector.memset(cst[:], 2.0)
        nc.vector.tensor_scalar(
            out=cst[:].rearrange("p (a x f) -> p a x f", a=4, x=8, f=4)[:, :, :, 2:4],
            in0=ancb[:].rearrange("p (a w) -> p a w", w=2).unsqueeze(2).to_broadcast([P, 4, 8, 2]),
            scalar1=8.0,
            scalar2=None,
            op0=ALU.mult,
        )
        factors_scalar(0, 1)
        for part in range(3):
            factors_vector(0, part)
        fix(0)
        sort(0)
        weave(0, nc.scalar.copy)
        prepare_w_weave()
        fix(1)
        sort(1)
        prepare_w_quant()

        for i in range(-1, PASSES):
            n_next = (i + 3) // 2
            new_image = i >= 1 and i % 2 == 1 and n_next < B
            if i == 0:
                factors_scalar(1, 2)
            if live(i + 1):
                transpose_d(i + 1)
            if new_image:
                factors_scalar(n_next, n_next + 1)
            if live(i):
                transpose_f(i)
            if i == 0:
                for part in range(3):
                    factors_vector(1, part)
                fix(2)
            if live(i + 1):
                q_b[i + 1] = quantize(grp_b[i + 1], E5, "b")
            if new_image:
                factors_vector(n_next, 0)
            if live(i + 2) and i >= 0:
                sort(i + 2)
            if new_image:
                factors_vector(n_next, 1)
            if live(i):
                q_f[i] = quantize(grp_f[i], E4, "f")
            if new_image:
                factors_vector(n_next, 2)
            if live(i):
                q_a[i] = quantize(grp_a[i], E5, "a")
            if live(i):
                mm0(i)
            if live(i + 3) and i >= 0:
                fix(i + 3)
            if live(i + 1) and i >= 0:
                weave(i + 1, nc.vector.tensor_copy)
            if i + 1 + G_BUFS < PASSES:
                load_g(i + 1 + G_BUFS)
            if i % 2 == 1 and live(i) and i // 2 + F_BUFS < B:
                load_f(i // 2 + F_BUFS)
        for a in range(4):
            mm1(PASSES - 1, a)
        for a in range(4):
            evacuate_out1(a, nc.vector.tensor_copy if a % 2 == 0 else nc.scalar.copy)
